import numpy as np
import ml_dtypes


def mxq(x, axis, fmt="e4m3"):
    dtype, down = {"e4m3": (ml_dtypes.float8_e4m3fn, 7), "e5m2": (ml_dtypes.float8_e5m2, 14)}[fmt]
    v = np.moveaxis(np.asarray(x, np.float32).astype(ml_dtypes.bfloat16).astype(np.float64), axis, -1)
    blocks = v.reshape(v.shape[:-1] + (-1, 32))
    amax = np.abs(blocks).max(-1, keepdims=True)
    byte = np.maximum(np.where(amax > 0, np.frexp(amax)[1] - 1 + 127, 0) - down, 1)
    scale = np.exp2(byte - 127.0)
    codes = (blocks / scale).astype(np.float32).astype(dtype).astype(np.float64)
    return np.moveaxis((codes * scale).reshape(v.shape), -1, axis)


WIDE = False


def mx_kscale(k):
    if not WIDE:
        return np.ones(k)
    levels = np.array([10, -10, 5, -5, 0])
    if k % 512:
        return np.exp2(np.random.permutation(np.resize(levels, k // 32))).repeat(32)
    a = np.empty((k // 512, 16))
    for p in range(k // 512):
        a[p, :8] = np.random.permutation(np.resize(levels, 8))
        for g in range(8):
            far = levels[np.abs(levels - a[p, g]) >= 10]
            a[p, g + 8] = far[np.random.randint(len(far))]
    return np.exp2(a.ravel()).repeat(32)


BF16 = ml_dtypes.bfloat16


def bf(x):
    return np.asarray(x, np.float32).astype(BF16)


def f64(x):
    return np.asarray(x).astype(np.float64)


B, S, D_IN, D_OUT = 8, 2048, 512, 128


def relative_shift(x):
    b, s, d = x.shape
    padded = np.concatenate([np.zeros((b, 1, d)), x], axis=1).reshape(s + 1, b, d)
    return padded[1:].reshape(b, s, d)


def setup_inputs():
    s = mx_kscale(D_IN)
    return {"pos_embed": bf(np.random.standard_normal((B, S, D_IN)) * s),
            "W_r": bf(np.random.standard_normal((D_OUT, D_IN)) * 1.2 / np.sqrt(D_IN) / s[None, :]),
            "b_r": bf(np.random.standard_normal(D_OUT) * 0.3)}


def reference(pos_embed, W_r, b_r):
    shifted = relative_shift(f64(pos_embed))
    return (mxq(shifted, 2, "e4m3") @ mxq(f64(W_r), 1, "e4m3").T) + f64(b_r)

@@ -1,0 +1,175 @@
+from contextlib import ExitStack
+
+import concourse.mybir as mybir
+from concourse.masks import make_identity
+
+BF16 = mybir.dt.bfloat16
+F32 = mybir.dt.float32
+U32 = mybir.dt.uint32
+U8 = mybir.dt.uint8
+FP8X4 = mybir.dt.float8_e4m3fn_x4
+
+P = 128
+BATCHES = 8
+SEQ = 2048
+D_IN = 512
+D_OUT = 128
+PACK = 4
+BANK = 512
+
+HALVES = D_IN // 2 // P
+TILES = SEQ // P
+GROUP = 8
+GROUPS = TILES // GROUP
+FLIPPED_TILES = BANK // (HALVES * P)
+PRODUCT_TILES = BANK // D_OUT
+
+ZERO_ROWS = BATCHES - 1
+LEFT_ROWS = SEQ - ZERO_ROWS - (TILES - 1) * P
+assert LEFT_ROWS + ZERO_ROWS == P
+
+FLOPS = 2 * BATCHES * SEQ * D_IN * D_OUT
+
+
+def transpose_row_tile(nc, identity, flipped, row_tile):
+    words = row_tile.bitcast(F32)
+    for u in range(HALVES):
+        nc.tensor.transpose(flipped[:, u, :], words[:, u::HALVES], identity)
+
+
+def tile_relativemultiheadattention_pa_t_kernel(tc, pos_embed, W_r, b_r, out):
+    nc = tc.nc
+    pos_rows = pos_embed.flatten_outer_dims()
+    out_rows = out.flatten_outer_dims()
+
+    def whole_tiles(b):
+        return TILES - 1 if b == 0 else TILES
+
+    def first_row(b):
+        return ZERO_ROWS if b == 0 else SEQ * b
+
+    def batch_source(b):
+        rows = pos_rows[first_row(b) : first_row(b) + whole_tiles(b) * P, :]
+        return rows.rearrange("(p t) k -> p t k", t=whole_tiles(b))
+
+    def batch_target(b):
+        first = first_row(b) + b - ZERO_ROWS
+        rows = out_rows[first : first + whole_tiles(b) * P, :]
+        return rows.rearrange("(p t) d -> p t d", t=whole_tiles(b))
+
+    left_source = pos_rows[SEQ - LEFT_ROWS : SEQ, :]
+    left_target = out_rows[SEQ - ZERO_ROWS - LEFT_ROWS : SEQ - ZERO_ROWS, :]
+    zero_target = out_rows[SEQ - ZERO_ROWS :, :].rearrange("(i r) d -> i r d", r=SEQ + 1)[:, 0, :]
+
+    with ExitStack() as ctx:
+        consts = ctx.enter_context(tc.tile_pool(name="consts", bufs=1))
+        x_pool = ctx.enter_context(tc.tile_pool(name="x", bufs=BATCHES))
+        grouped_pool = ctx.enter_context(tc.tile_pool(name="grouped", bufs=2))
+        mx_pool = ctx.enter_context(tc.tile_pool(name="mx", bufs=2))
+        keys_pool = ctx.enter_context(tc.tile_pool(name="keys", bufs=BATCHES))
+        flipped_pool = ctx.enter_context(tc.psum_pool(name="flipped", bufs=4))
+        product_pool = ctx.enter_context(tc.psum_pool(name="product", bufs=4))
+        ctx.enter_context(tc.manual_schedule())
+
+        w_raw = consts.tile([P, D_IN], BF16)
+        nc.scalar.dma_start(out=w_raw[:], in_=W_r)
+        bias_rows = consts.tile([P, D_OUT], BF16)
+        nc.vector.memset(bias_rows[:], 0.0)
+        nc.scalar.dma_start(out=bias_rows[0:1, :], in_=b_r.unsqueeze(0))
+
+        x_batches = []
+        for b in range(BATCHES):
+            x_batch = x_pool.tile([P, TILES, D_IN], BF16, name="x_batch")
+            x_batches.append(x_batch)
+            step = GROUP if b == 0 else TILES
+            for first in range(0, TILES, step):
+                last = min(first + step, whole_tiles(b))
+                nc.sync.dma_start(out=x_batch[:, first:last, :], in_=batch_source(b)[:, first:last, :])
+            if b == 0:
+                nc.vector.memset(x_batch[:, TILES - 1, :], 0.0)
+                nc.sync.dma_start(out=x_batch[0:LEFT_ROWS, TILES - 1, :], in_=left_source)
+
+        identity = consts.tile([P, P], F32)
+        make_identity(nc, identity[:])
+
+        w_flipped = flipped_pool.tile([P, FLIPPED_TILES, HALVES, P], F32, name="flipped")
+        transpose_row_tile(nc, identity[:], w_flipped[:, 0], w_raw[:])
+        w_grouped = consts.tile([P, D_OUT * PACK], BF16, align_bytes=64)
+        nc.scalar.copy(
+            out=w_grouped[:].bitcast(F32).rearrange("p (r u) -> p r u", u=HALVES),
+            in_=w_flipped[:, 0].rearrange("p u r -> p r u"),
+        )
+        w_codes = consts.tile([P, D_OUT], U32, align_bytes=64)
+        w_scales = consts.tile([P, D_OUT], U8, align_bytes=64)
+        nc.vector.quantize_mx(out=w_codes[:].bitcast(FP8X4), scales=w_scales[:], in_=w_grouped[:])
+
+        ones = consts.tile([P, P], BF16)
+        nc.vector.memset(ones[:], 1.0)
+        bias_product = product_pool.tile([P, PRODUCT_TILES, D_OUT], F32, name="product")
+        nc.tensor.matmul(out=bias_product[:, 0, :], lhsT=ones[:], rhs=bias_rows[:], start=True, stop=True)
+        bias = consts.tile([P, D_OUT], F32)
+        nc.vector.tensor_copy(out=bias[:], in_=bias_product[:, 0, :])
+
+        def flip_group(g):
+            x_batch = x_batches[g // GROUPS]
+            first = (g % GROUPS) * GROUP
+            grouped = grouped_pool.tile([P, GROUP * P * PACK], BF16, align_bytes=64, name="grouped")
+            grouped_words = grouped[:].bitcast(F32).rearrange("p (t r u) -> p t r u", r=P, u=HALVES)
+            for t in range(0, GROUP, FLIPPED_TILES):
+                flipped = flipped_pool.tile([P, FLIPPED_TILES, HALVES, P], F32, name="flipped")
+                for i in range(FLIPPED_TILES):
+                    transpose_row_tile(nc, identity[:], flipped[:, i], x_batch[:, first + t + i, :])
+                nc.scalar.copy(
+                    out=grouped_words[:, t : t + FLIPPED_TILES],
+                    in_=flipped[:].rearrange("p i u r -> p i r u"),
+                )
+            return grouped
+
+        def quantise_group(grouped):
+            codes = mx_pool.tile([P, GROUP * P], U32, align_bytes=64, name="codes")
+            scales = mx_pool.tile([P, GROUP * P], U8, align_bytes=64, name="scales")
+            nc.vector.quantize_mx(out=codes[:].bitcast(FP8X4), scales=scales[:], in_=grouped[:])
+            return codes, scales
+
+        keys_batches = []
+
+        def multiply_group(g, codes, scales):
+            b = g // GROUPS
+            first = (g % GROUPS) * GROUP
+            if first == 0:
+                keys_batches.append(keys_pool.tile([P, TILES, D_OUT], F32, name="keys"))
+            keys = keys_batches[b]
+            for t in range(0, GROUP, PRODUCT_TILES):
+                product = product_pool.tile([P, PRODUCT_TILES, D_OUT], F32, name="product")
+                for i in range(PRODUCT_TILES):
+                    rows = slice((t + i) * P, (t + i + 1) * P)
+                    nc.tensor.matmul_mx(
+                        out=product[:, i, :],
+                        lhsT=codes[:, rows].bitcast(FP8X4),
+                        lhsT_scale=scales[:, rows],
+                        rhs=w_codes[:].bitcast(FP8X4),
+                        rhs_scale=w_scales[:],
+                        start=True,
+                        stop=True,
+                    )
+                nc.vector.tensor_add(
+                    out=keys[:, first + t : first + t + PRODUCT_TILES, :],
+                    in0=product[:],
+                    in1=bias[:].unsqueeze(1).to_broadcast([P, PRODUCT_TILES, D_OUT]),
+                )
+            if first + GROUP == TILES:
+                nc.sync.dma_start(out=batch_target(b), in_=keys[:, 0 : whole_tiles(b), :])
+                if b == 0:
+                    nc.sync.dma_start(out=left_target, in_=keys[0:LEFT_ROWS, TILES - 1, :])
+                    nc.sync.dma_start(out=zero_target, in_=keys[LEFT_ROWS:P, TILES - 1, :])
+
+        n_groups = BATCHES * GROUPS
+        flipped_groups = {}
+        quantised_groups = {}
+        for g in range(n_groups + 2):
+            if g < n_groups:
+                flipped_groups[g] = flip_group(g)
+            if 1 <= g <= n_groups:
+                quantised_groups[g - 1] = quantise_group(flipped_groups[g - 1])
+            if g >= 2:
+                multiply_group(g - 2, *quantised_groups[g - 2])

@@ -20,7 +20,8 @@ BANK = 512
 HALVES = D_IN // 2 // P
 TILES = SEQ // P
 GROUP = 8
-GROUPS = TILES // GROUP
+GROUP_WIDTHS = {0: (4, 4, 8), BATCHES - 1: (8, 4, 4)}
+SPREAD_SHARE = 4
 FLIPPED_TILES = BANK // (HALVES * P)
 PRODUCT_TILES = BANK // D_OUT
 
@@ -35,6 +36,11 @@ def transpose_row_tile(nc, identity, flipped, row_tile):
     words = row_tile.bitcast(F32)
     for u in range(HALVES):
         nc.tensor.transpose(flipped[:, u, :], words[:, u::HALVES], identity)
+
+
+def transpose_spread_tile(nc, identity, flipped, spread, t):
+    for u in range(HALVES):
+        nc.tensor.transpose(flipped[:, u, :], spread[:, u, t * P : (t + 1) * P], identity)
 
 
 def tile_relativemultiheadattention_pa_t_kernel(tc, pos_embed, W_r, b_r, out):
@@ -64,7 +70,8 @@ def tile_relativemultiheadattention_pa_t_kernel(tc, pos_embed, W_r, b_r, out):
     with ExitStack() as ctx:
         consts = ctx.enter_context(tc.tile_pool(name="consts", bufs=1))
         x_pool = ctx.enter_context(tc.tile_pool(name="x", bufs=BATCHES))
-        grouped_pool = ctx.enter_context(tc.tile_pool(name="grouped", bufs=2))
+        grouped_pool = ctx.enter_context(tc.tile_pool(name="grouped", bufs=3))
+        spread_pool = ctx.enter_context(tc.tile_pool(name="spread", bufs=2))
         mx_pool = ctx.enter_context(tc.tile_pool(name="mx", bufs=2))
         keys_pool = ctx.enter_context(tc.tile_pool(name="keys", bufs=BATCHES))
         flipped_pool = ctx.enter_context(tc.psum_pool(name="flipped", bufs=4))
@@ -72,7 +79,8 @@ def tile_relativemultiheadattention_pa_t_kernel(tc, pos_embed, W_r, b_r, out):
         ctx.enter_context(tc.manual_schedule())
 
         w_raw = consts.tile([P, D_IN], BF16)
-        nc.scalar.dma_start(out=w_raw[:], in_=W_r)
+        ones = consts.tile([P, P], BF16)
+        nc.vector.memset(ones[:], 1.0)
         bias_rows = consts.tile([P, D_OUT], BF16)
         nc.vector.memset(bias_rows[:], 0.0)
         nc.scalar.dma_start(out=bias_rows[0:1, :], in_=b_r.unsqueeze(0))
@@ -81,10 +89,12 @@ def tile_relativemultiheadattention_pa_t_kernel(tc, pos_embed, W_r, b_r, out):
         for b in range(BATCHES):
             x_batch = x_pool.tile([P, TILES, D_IN], BF16, name="x_batch")
             x_batches.append(x_batch)
-            step = GROUP if b == 0 else TILES
+            step = {0: TILES // 4, 1: TILES // 2}.get(b, TILES)
             for first in range(0, TILES, step):
                 last = min(first + step, whole_tiles(b))
                 nc.sync.dma_start(out=x_batch[:, first:last, :], in_=batch_source(b)[:, first:last, :])
+                if b == 0 and first == 0:
+                    nc.sync.dma_start(out=w_raw[:], in_=W_r)
             if b == 0:
                 nc.vector.memset(x_batch[:, TILES - 1, :], 0.0)
                 nc.sync.dma_start(out=x_batch[0:LEFT_ROWS, TILES - 1, :], in_=left_source)
@@ -92,54 +102,76 @@ def tile_relativemultiheadattention_pa_t_kernel(tc, pos_embed, W_r, b_r, out):
         identity = consts.tile([P, P], F32)
         make_identity(nc, identity[:])
 
-        w_flipped = flipped_pool.tile([P, FLIPPED_TILES, HALVES, P], F32, name="flipped")
-        transpose_row_tile(nc, identity[:], w_flipped[:, 0], w_raw[:])
-        w_grouped = consts.tile([P, D_OUT * PACK], BF16, align_bytes=64)
-        nc.scalar.copy(
-            out=w_grouped[:].bitcast(F32).rearrange("p (r u) -> p r u", u=HALVES),
-            in_=w_flipped[:, 0].rearrange("p u r -> p r u"),
-        )
         w_codes = consts.tile([P, D_OUT], U32, align_bytes=64)
         w_scales = consts.tile([P, D_OUT], U8, align_bytes=64)
-        nc.vector.quantize_mx(out=w_codes[:].bitcast(FP8X4), scales=w_scales[:], in_=w_grouped[:])
-
-        ones = consts.tile([P, P], BF16)
-        nc.vector.memset(ones[:], 1.0)
-        bias_product = product_pool.tile([P, PRODUCT_TILES, D_OUT], F32, name="product")
-        nc.tensor.matmul(out=bias_product[:, 0, :], lhsT=ones[:], rhs=bias_rows[:], start=True, stop=True)
         bias = consts.tile([P, D_OUT], F32)
-        nc.vector.tensor_copy(out=bias[:], in_=bias_product[:, 0, :])
 
-        def flip_group(g):
-            x_batch = x_batches[g // GROUPS]
-            first = (g % GROUPS) * GROUP
-            grouped = grouped_pool.tile([P, GROUP * P * PACK], BF16, align_bytes=64, name="grouped")
+        def prepare_weights():
+            w_flipped = flipped_pool.tile([P, FLIPPED_TILES, HALVES, P], F32, name="flipped")
+            transpose_row_tile(nc, identity[:], w_flipped[:, 0], w_raw[:])
+            w_grouped = consts.tile([P, D_OUT * PACK], BF16, align_bytes=64, name="w_grouped")
+            nc.scalar.copy(
+                out=w_grouped[:].bitcast(F32).rearrange("p (r u) -> p r u", u=HALVES),
+                in_=w_flipped[:, 0].rearrange("p u r -> p r u"),
+            )
+            nc.vector.quantize_mx(out=w_codes[:].bitcast(FP8X4), scales=w_scales[:], in_=w_grouped[:])
+
+            bias_product = product_pool.tile([P, PRODUCT_TILES, D_OUT], F32, name="product")
+            nc.tensor.matmul(out=bias_product[:, 0, :], lhsT=ones[:], rhs=bias_rows[:], start=True, stop=True)
+            nc.vector.tensor_copy(out=bias[:], in_=bias_product[:, 0, :])
+
+        groups = []
+        for b in range(BATCHES):
+            first = 0
+            for width in GROUP_WIDTHS.get(b, (GROUP, GROUP)):
+                groups.append((b, first, width))
+                first += width
+
+        def spread_group(g):
+            b, first, width = groups[g]
+            count = width // SPREAD_SHARE
+            row_tiles = x_batches[b][:, first + width - count : first + width, :]
+            spread = spread_pool.tile([P, HALVES, count * P], F32, name="spread")
+            nc.vector.tensor_copy(
+                out=spread[:],
+                in_=row_tiles.rearrange("p t k -> p (t k)").bitcast(F32).rearrange("p (w u) -> p u w", u=HALVES),
+            )
+            return spread
+
+        def flip_group(g, spread):
+            b, first, width = groups[g]
+            x_batch = x_batches[b]
+            plain = width if spread is None else width - width // SPREAD_SHARE
+            grouped = grouped_pool.tile([P, width * P * PACK], BF16, align_bytes=64, name="grouped")
             grouped_words = grouped[:].bitcast(F32).rearrange("p (t r u) -> p t r u", r=P, u=HALVES)
-            for t in range(0, GROUP, FLIPPED_TILES):
+            for t in range(0, width, FLIPPED_TILES):
                 flipped = flipped_pool.tile([P, FLIPPED_TILES, HALVES, P], F32, name="flipped")
                 for i in range(FLIPPED_TILES):
-                    transpose_row_tile(nc, identity[:], flipped[:, i], x_batch[:, first + t + i, :])
+                    if t + i >= plain:
+                        transpose_spread_tile(nc, identity[:], flipped[:, i], spread, t + i - plain)
+                    else:
+                        transpose_row_tile(nc, identity[:], flipped[:, i], x_batch[:, first + t + i, :])
                 nc.scalar.copy(
                     out=grouped_words[:, t : t + FLIPPED_TILES],
                     in_=flipped[:].rearrange("p i u r -> p i r u"),
                 )
             return grouped
 
-        def quantise_group(grouped):
-            codes = mx_pool.tile([P, GROUP * P], U32, align_bytes=64, name="codes")
-            scales = mx_pool.tile([P, GROUP * P], U8, align_bytes=64, name="scales")
+        def quantise_group(g, grouped):
+            width = groups[g][2]
+            codes = mx_pool.tile([P, width * P], U32, align_bytes=64, name="codes")
+            scales = mx_pool.tile([P, width * P], U8, align_bytes=64, name="scales")
             nc.vector.quantize_mx(out=codes[:].bitcast(FP8X4), scales=scales[:], in_=grouped[:])
             return codes, scales
 
         keys_batches = []
 
         def multiply_group(g, codes, scales):
-            b = g // GROUPS
-            first = (g % GROUPS) * GROUP
+            b, first, width = groups[g]
             if first == 0:
                 keys_batches.append(keys_pool.tile([P, TILES, D_OUT], F32, name="keys"))
             keys = keys_batches[b]
-            for t in range(0, GROUP, PRODUCT_TILES):
+            for t in range(0, width, PRODUCT_TILES):
                 product = product_pool.tile([P, PRODUCT_TILES, D_OUT], F32, name="product")
                 for i in range(PRODUCT_TILES):
                     rows = slice((t + i) * P, (t + i + 1) * P)
@@ -157,19 +189,27 @@ def tile_relativemultiheadattention_pa_t_kernel(tc, pos_embed, W_r, b_r, out):
                     in0=product[:],
                     in1=bias[:].unsqueeze(1).to_broadcast([P, PRODUCT_TILES, D_OUT]),
                 )
-            if first + GROUP == TILES:
+            if b == BATCHES - 1:
+                done = slice(first, first + width)
+                nc.sync.dma_start(out=batch_target(b)[:, done, :], in_=keys[:, done, :])
+            elif first + width == TILES:
                 nc.sync.dma_start(out=batch_target(b), in_=keys[:, 0 : whole_tiles(b), :])
                 if b == 0:
                     nc.sync.dma_start(out=left_target, in_=keys[0:LEFT_ROWS, TILES - 1, :])
                     nc.sync.dma_start(out=zero_target, in_=keys[LEFT_ROWS:P, TILES - 1, :])
 
-        n_groups = BATCHES * GROUPS
+        n_groups = len(groups)
+        spread_groups = {0: None}
         flipped_groups = {}
         quantised_groups = {}
         for g in range(n_groups + 2):
+            if g + 1 < n_groups:
+                spread_groups[g + 1] = spread_group(g + 1)
             if g < n_groups:
-                flipped_groups[g] = flip_group(g)
+                flipped_groups[g] = flip_group(g, spread_groups[g])
+            if g == 0:
+                prepare_weights()
             if 1 <= g <= n_groups:
-                quantised_groups[g - 1] = quantise_group(flipped_groups[g - 1])
+                quantised_groups[g - 1] = quantise_group(g - 1, flipped_groups[g - 1])
             if g >= 2:
                 multiply_group(g - 2, *quantised_groups[g - 2])

@@ -21,7 +21,8 @@ HALVES = D_IN // 2 // P
 TILES = SEQ // P
 GROUP = 8
 GROUP_WIDTHS = {0: (4, 4, 8), BATCHES - 1: (8, 4, 4)}
-SPREAD_SHARE = 4
+VECTOR_SORTS = {8: 2, 4: 1}
+SCALAR_SORTS = {8: 1, 4: 1}
 FLIPPED_TILES = BANK // (HALVES * P)
 PRODUCT_TILES = BANK // D_OUT
 
@@ -69,13 +70,13 @@ def tile_relativemultiheadattention_pa_t_kernel(tc, pos_embed, W_r, b_r, out):
 
     with ExitStack() as ctx:
         consts = ctx.enter_context(tc.tile_pool(name="consts", bufs=1))
-        x_pool = ctx.enter_context(tc.tile_pool(name="x", bufs=BATCHES))
+        x_pool = ctx.enter_context(tc.tile_pool(name="x", bufs=BATCHES - 1))
         grouped_pool = ctx.enter_context(tc.tile_pool(name="grouped", bufs=3))
         spread_pool = ctx.enter_context(tc.tile_pool(name="spread", bufs=2))
         mx_pool = ctx.enter_context(tc.tile_pool(name="mx", bufs=2))
         keys_pool = ctx.enter_context(tc.tile_pool(name="keys", bufs=BATCHES))
-        flipped_pool = ctx.enter_context(tc.psum_pool(name="flipped", bufs=4))
-        product_pool = ctx.enter_context(tc.psum_pool(name="product", bufs=4))
+        flipped_pool = ctx.enter_context(tc.psum_pool(name="flipped", bufs=6))
+        product_pool = ctx.enter_context(tc.psum_pool(name="product", bufs=2))
         ctx.enter_context(tc.manual_schedule())
 
         w_raw = consts.tile([P, D_IN], BF16)
@@ -89,7 +90,7 @@ def tile_relativemultiheadattention_pa_t_kernel(tc, pos_embed, W_r, b_r, out):
         for b in range(BATCHES):
             x_batch = x_pool.tile([P, TILES, D_IN], BF16, name="x_batch")
             x_batches.append(x_batch)
-            step = {0: TILES // 4, 1: TILES // 2}.get(b, TILES)
+            step = {0: TILES // 4, 1: TILES // 2, 2: TILES // 2}.get(b, TILES)
             for first in range(0, TILES, step):
                 last = min(first + step, whole_tiles(b))
                 nc.sync.dma_start(out=x_batch[:, first:last, :], in_=batch_source(b)[:, first:last, :])
@@ -127,28 +128,45 @@ def tile_relativemultiheadattention_pa_t_kernel(tc, pos_embed, W_r, b_r, out):
                 groups.append((b, first, width))
                 first += width
 
-        def spread_group(g):
+        def sorted_from(g):
+            width = groups[g][2]
+            by_vector = width - VECTOR_SORTS[width]
+            return by_vector - SCALAR_SORTS[width], by_vector
+
+        def sort_words(g, first_tile, last_tile, spread, copy):
             b, first, width = groups[g]
-            count = width // SPREAD_SHARE
-            row_tiles = x_batches[b][:, first + width - count : first + width, :]
-            spread = spread_pool.tile([P, HALVES, count * P], F32, name="spread")
-            nc.vector.tensor_copy(
+            row_tiles = x_batches[b][:, first + first_tile : first + last_tile, :]
+            copy(
                 out=spread[:],
                 in_=row_tiles.rearrange("p t k -> p (t k)").bitcast(F32).rearrange("p (w u) -> p u w", u=HALVES),
             )
+
+        def sort_on_scalar(g):
+            by_scalar, by_vector = sorted_from(g)
+            spread = spread_pool.tile([P, HALVES, (by_vector - by_scalar) * P], F32, name="scalar_spread")
+            sort_words(g, by_scalar, by_vector, spread, nc.scalar.copy)
             return spread
 
-        def flip_group(g, spread):
+        def sort_on_vector(g):
+            width = groups[g][2]
+            by_vector = sorted_from(g)[1]
+            spread = spread_pool.tile([P, HALVES, (width - by_vector) * P], F32, name="vector_spread")
+            sort_words(g, by_vector, width, spread, nc.vector.tensor_copy)
+            return spread
+
+        def flip_group(g, scalar_spread, vector_spread):
             b, first, width = groups[g]
             x_batch = x_batches[b]
-            plain = width if spread is None else width - width // SPREAD_SHARE
+            by_scalar, by_vector = sorted_from(g) if g else (width, width)
             grouped = grouped_pool.tile([P, width * P * PACK], BF16, align_bytes=64, name="grouped")
             grouped_words = grouped[:].bitcast(F32).rearrange("p (t r u) -> p t r u", r=P, u=HALVES)
             for t in range(0, width, FLIPPED_TILES):
                 flipped = flipped_pool.tile([P, FLIPPED_TILES, HALVES, P], F32, name="flipped")
                 for i in range(FLIPPED_TILES):
-                    if t + i >= plain:
-                        transpose_spread_tile(nc, identity[:], flipped[:, i], spread, t + i - plain)
+                    if t + i >= by_vector:
+                        transpose_spread_tile(nc, identity[:], flipped[:, i], vector_spread, t + i - by_vector)
+                    elif t + i >= by_scalar:
+                        transpose_spread_tile(nc, identity[:], flipped[:, i], scalar_spread, t + i - by_scalar)
                     else:
                         transpose_row_tile(nc, identity[:], flipped[:, i], x_batch[:, first + t + i, :])
                 nc.scalar.copy(
@@ -199,17 +217,20 @@ def tile_relativemultiheadattention_pa_t_kernel(tc, pos_embed, W_r, b_r, out):
                     nc.sync.dma_start(out=zero_target, in_=keys[LEFT_ROWS:P, TILES - 1, :])
 
         n_groups = len(groups)
-        spread_groups = {0: None}
+        scalar_spreads = {0: None}
+        vector_spreads = {0: None}
         flipped_groups = {}
         quantised_groups = {}
         for g in range(n_groups + 2):
-            if g + 1 < n_groups:
-                spread_groups[g + 1] = spread_group(g + 1)
             if g < n_groups:
-                flipped_groups[g] = flip_group(g, spread_groups[g])
-            if g == 0:
-                prepare_weights()
+                flipped_groups[g] = flip_group(g, scalar_spreads[g], vector_spreads[g])
+            if g + 1 < n_groups:
+                scalar_spreads[g + 1] = sort_on_scalar(g + 1)
             if 1 <= g <= n_groups:
                 quantised_groups[g - 1] = quantise_group(g - 1, flipped_groups[g - 1])
+            if g + 1 < n_groups:
+                vector_spreads[g + 1] = sort_on_vector(g + 1)
+            if g == 0:
+                prepare_weights()
             if g >= 2:
                 multiply_group(g - 2, *quantised_groups[g - 2])

@@ -17,6 +17,7 @@ D_OUT = 128
 PACK = 4
 BANK = 512
 
+RUN = 8
 HALVES = D_IN // 2 // P
 TILES = SEQ // P
 GROUP = 8
@@ -39,7 +40,15 @@ def transpose_row_tile(nc, identity, flipped, row_tile):
         nc.tensor.transpose(flipped[:, u, :], words[:, u::HALVES], identity)
 
 
-def transpose_spread_tile(nc, identity, flipped, spread, t):
+def sort_words(copy, spread, row_tiles):
+    words = row_tiles.rearrange("p t k -> p (t k)").bitcast(F32)
+    copy(
+        out=spread.rearrange("p u (n i) -> p u n i", i=RUN),
+        in_=words.rearrange("p (n u i) -> p u n i", u=HALVES, i=RUN),
+    )
+
+
+def transpose_sorted_tile(nc, identity, flipped, spread, t):
     for u in range(HALVES):
         nc.tensor.transpose(flipped[:, u, :], spread[:, u, t * P : (t + 1) * P], identity)
 
@@ -86,6 +95,7 @@ def tile_relativemultiheadattention_pa_t_kernel(tc, pos_embed, W_r, b_r, out):
         nc.vector.memset(bias_rows[:], 0.0)
         nc.scalar.dma_start(out=bias_rows[0:1, :], in_=b_r.unsqueeze(0))
 
+        nc.sync.dma_start(out=w_raw[:], in_=W_r)
         x_batches = []
         for b in range(BATCHES):
             x_batch = x_pool.tile([P, TILES, D_IN], BF16, name="x_batch")
@@ -94,8 +104,6 @@ def tile_relativemultiheadattention_pa_t_kernel(tc, pos_embed, W_r, b_r, out):
             for first in range(0, TILES, step):
                 last = min(first + step, whole_tiles(b))
                 nc.sync.dma_start(out=x_batch[:, first:last, :], in_=batch_source(b)[:, first:last, :])
-                if b == 0 and first == 0:
-                    nc.sync.dma_start(out=w_raw[:], in_=W_r)
             if b == 0:
                 nc.vector.memset(x_batch[:, TILES - 1, :], 0.0)
                 nc.sync.dma_start(out=x_batch[0:LEFT_ROWS, TILES - 1, :], in_=left_source)
@@ -103,20 +111,24 @@ def tile_relativemultiheadattention_pa_t_kernel(tc, pos_embed, W_r, b_r, out):
         identity = consts.tile([P, P], F32)
         make_identity(nc, identity[:])
 
-        w_codes = consts.tile([P, D_OUT], U32, align_bytes=64)
-        w_scales = consts.tile([P, D_OUT], U8, align_bytes=64)
+        w_codes = consts.tile([P, 2 * D_OUT], U32, align_bytes=64)
+        w_scales = consts.tile([P, 2 * D_OUT], U8, align_bytes=64)
         bias = consts.tile([P, D_OUT], F32)
 
         def prepare_weights():
+            w_spread = consts.tile([P, HALVES, P], F32, name="w_spread")
+            sort_words(nc.vector.tensor_copy, w_spread[:], w_raw[:].unsqueeze(1))
             w_flipped = flipped_pool.tile([P, FLIPPED_TILES, HALVES, P], F32, name="flipped")
             transpose_row_tile(nc, identity[:], w_flipped[:, 0], w_raw[:])
-            w_grouped = consts.tile([P, D_OUT * PACK], BF16, align_bytes=64, name="w_grouped")
+            transpose_sorted_tile(nc, identity[:], w_flipped[:, 1], w_spread[:], 0)
+            w_grouped = consts.tile([P, 2 * D_OUT * PACK], BF16, align_bytes=64, name="w_grouped")
             nc.scalar.copy(
-                out=w_grouped[:].bitcast(F32).rearrange("p (r u) -> p r u", u=HALVES),
-                in_=w_flipped[:, 0].rearrange("p u r -> p r u"),
+                out=w_grouped[:].bitcast(F32).rearrange("p (i r u) -> p i r u", i=2, u=HALVES),
+                in_=w_flipped[:].rearrange("p i u r -> p i r u"),
             )
             nc.vector.quantize_mx(out=w_codes[:].bitcast(FP8X4), scales=w_scales[:], in_=w_grouped[:])
 
+        def prepare_bias():
             bias_product = product_pool.tile([P, PRODUCT_TILES, D_OUT], F32, name="product")
             nc.tensor.matmul(out=bias_product[:, 0, :], lhsT=ones[:], rhs=bias_rows[:], start=True, stop=True)
             nc.vector.tensor_copy(out=bias[:], in_=bias_product[:, 0, :])
@@ -127,31 +139,25 @@ def tile_relativemultiheadattention_pa_t_kernel(tc, pos_embed, W_r, b_r, out):
             for width in GROUP_WIDTHS.get(b, (GROUP, GROUP)):
                 groups.append((b, first, width))
                 first += width
+        n_groups = len(groups)
 
         def sorted_from(g):
             width = groups[g][2]
-            by_vector = width - VECTOR_SORTS[width]
+            by_vector = width - (VECTOR_SORTS[width] if g < n_groups - 2 else 0)
             return by_vector - SCALAR_SORTS[width], by_vector
 
-        def sort_words(g, first_tile, last_tile, spread, copy):
-            b, first, width = groups[g]
-            row_tiles = x_batches[b][:, first + first_tile : first + last_tile, :]
-            copy(
-                out=spread[:],
-                in_=row_tiles.rearrange("p t k -> p (t k)").bitcast(F32).rearrange("p (w u) -> p u w", u=HALVES),
-            )
-
         def sort_on_scalar(g):
+            b, first, width = groups[g]
             by_scalar, by_vector = sorted_from(g)
             spread = spread_pool.tile([P, HALVES, (by_vector - by_scalar) * P], F32, name="scalar_spread")
-            sort_words(g, by_scalar, by_vector, spread, nc.scalar.copy)
+            sort_words(nc.scalar.copy, spread[:], x_batches[b][:, first + by_scalar : first + by_vector, :])
             return spread
 
         def sort_on_vector(g):
-            width = groups[g][2]
+            b, first, width = groups[g]
             by_vector = sorted_from(g)[1]
             spread = spread_pool.tile([P, HALVES, (width - by_vector) * P], F32, name="vector_spread")
-            sort_words(g, by_vector, width, spread, nc.vector.tensor_copy)
+            sort_words(nc.vector.tensor_copy, spread[:], x_batches[b][:, first + by_vector : first + width, :])
             return spread
 
         def flip_group(g, scalar_spread, vector_spread):
@@ -164,9 +170,9 @@ def tile_relativemultiheadattention_pa_t_kernel(tc, pos_embed, W_r, b_r, out):
                 flipped = flipped_pool.tile([P, FLIPPED_TILES, HALVES, P], F32, name="flipped")
                 for i in range(FLIPPED_TILES):
                     if t + i >= by_vector:
-                        transpose_spread_tile(nc, identity[:], flipped[:, i], vector_spread, t + i - by_vector)
+                        transpose_sorted_tile(nc, identity[:], flipped[:, i], vector_spread, t + i - by_vector)
                     elif t + i >= by_scalar:
-                        transpose_spread_tile(nc, identity[:], flipped[:, i], scalar_spread, t + i - by_scalar)
+                        transpose_sorted_tile(nc, identity[:], flipped[:, i], scalar_spread, t + i - by_scalar)
                     else:
                         transpose_row_tile(nc, identity[:], flipped[:, i], x_batch[:, first + t + i, :])
                 nc.scalar.copy(
@@ -186,6 +192,7 @@ def tile_relativemultiheadattention_pa_t_kernel(tc, pos_embed, W_r, b_r, out):
 
         def multiply_group(g, codes, scales):
             b, first, width = groups[g]
+            by_scalar = sorted_from(g)[0] if g else width
             if first == 0:
                 keys_batches.append(keys_pool.tile([P, TILES, D_OUT], F32, name="keys"))
             keys = keys_batches[b]
@@ -193,12 +200,13 @@ def tile_relativemultiheadattention_pa_t_kernel(tc, pos_embed, W_r, b_r, out):
                 product = product_pool.tile([P, PRODUCT_TILES, D_OUT], F32, name="product")
                 for i in range(PRODUCT_TILES):
                     rows = slice((t + i) * P, (t + i + 1) * P)
+                    w_columns = slice(D_OUT, 2 * D_OUT) if t + i >= by_scalar else slice(0, D_OUT)
                     nc.tensor.matmul_mx(
                         out=product[:, i, :],
                         lhsT=codes[:, rows].bitcast(FP8X4),
                         lhsT_scale=scales[:, rows],
-                        rhs=w_codes[:].bitcast(FP8X4),
-                        rhs_scale=w_scales[:],
+                        rhs=w_codes[:, w_columns].bitcast(FP8X4),
+                        rhs_scale=w_scales[:, w_columns],
                         start=True,
                         stop=True,
                     )
@@ -216,7 +224,7 @@ def tile_relativemultiheadattention_pa_t_kernel(tc, pos_embed, W_r, b_r, out):
                     nc.sync.dma_start(out=left_target, in_=keys[0:LEFT_ROWS, TILES - 1, :])
                     nc.sync.dma_start(out=zero_target, in_=keys[LEFT_ROWS:P, TILES - 1, :])
 
-        n_groups = len(groups)
+        prepare_weights()
         scalar_spreads = {0: None}
         vector_spreads = {0: None}
         flipped_groups = {}
@@ -229,8 +237,8 @@ def tile_relativemultiheadattention_pa_t_kernel(tc, pos_embed, W_r, b_r, out):
             if 1 <= g <= n_groups:
                 quantised_groups[g - 1] = quantise_group(g - 1, flipped_groups[g - 1])
             if g + 1 < n_groups:
-                vector_spreads[g + 1] = sort_on_vector(g + 1)
-            if g == 0:
-                prepare_weights()
+                vector_spreads[g + 1] = sort_on_vector(g + 1) if g + 1 < n_groups - 2 else None
+            if g == 1:
+                prepare_bias()
             if g >= 2:
                 multiply_group(g - 2, *quantised_groups[g - 2])

@@ -27,9 +27,8 @@ SCALAR_SORTS = {8: 1, 4: 1}
 FLIPPED_TILES = BANK // (HALVES * P)
 PRODUCT_TILES = BANK // D_OUT
 
+LATE_LOADS = 2
 ZERO_ROWS = BATCHES - 1
-LEFT_ROWS = SEQ - ZERO_ROWS - (TILES - 1) * P
-assert LEFT_ROWS + ZERO_ROWS == P
 
 FLOPS = 2 * BATCHES * SEQ * D_IN * D_OUT
 
@@ -58,24 +57,15 @@ def tile_relativemultiheadattention_pa_t_kernel(tc, pos_embed, W_r, b_r, out):
     pos_rows = pos_embed.flatten_outer_dims()
     out_rows = out.flatten_outer_dims()
 
-    def whole_tiles(b):
-        return TILES - 1 if b == 0 else TILES
-
-    def first_row(b):
-        return ZERO_ROWS if b == 0 else SEQ * b
-
     def batch_source(b):
-        rows = pos_rows[first_row(b) : first_row(b) + whole_tiles(b) * P, :]
-        return rows.rearrange("(p t) k -> p t k", t=whole_tiles(b))
+        first = ZERO_ROWS if b == 0 else SEQ * b
+        return pos_rows[first : first + SEQ, :].rearrange("(p t) k -> p t k", t=TILES)
 
     def batch_target(b):
-        first = first_row(b) + b - ZERO_ROWS
-        rows = out_rows[first : first + whole_tiles(b) * P, :]
-        return rows.rearrange("(p t) d -> p t d", t=whole_tiles(b))
+        first = 0 if b == 0 else (SEQ + 1) * b - ZERO_ROWS
+        return out_rows[first : first + SEQ, :].rearrange("(p t) d -> p t d", t=TILES)
 
-    left_source = pos_rows[SEQ - LEFT_ROWS : SEQ, :]
-    left_target = out_rows[SEQ - ZERO_ROWS - LEFT_ROWS : SEQ - ZERO_ROWS, :]
-    zero_target = out_rows[SEQ - ZERO_ROWS :, :].rearrange("(i r) d -> i r d", r=SEQ + 1)[:, 0, :]
+    zero_target = out_rows[SEQ - ZERO_ROWS :, :].rearrange("(i r) d -> i r d", r=SEQ + 1)[1:, 0, :]
 
     with ExitStack() as ctx:
         consts = ctx.enter_context(tc.tile_pool(name="consts", bufs=1))
@@ -97,20 +87,19 @@ def tile_relativemultiheadattention_pa_t_kernel(tc, pos_embed, W_r, b_r, out):
 
         nc.sync.dma_start(out=w_raw[:], in_=W_r)
         x_batches = []
-        for b in range(BATCHES):
+
+        def load_batch(b):
             x_batch = x_pool.tile([P, TILES, D_IN], BF16, name="x_batch")
             x_batches.append(x_batch)
-            step = {0: TILES // 4, 1: TILES // 2, 2: TILES // 2}.get(b, TILES)
-            for first in range(0, TILES, step):
-                last = min(first + step, whole_tiles(b))
+            edges = {0: (0, 4, 8, TILES), 1: (0, 8, TILES)}.get(b, (0, TILES))
+            for first, last in zip(edges, edges[1:]):
                 nc.sync.dma_start(out=x_batch[:, first:last, :], in_=batch_source(b)[:, first:last, :])
-            if b == 0:
-                nc.vector.memset(x_batch[:, TILES - 1, :], 0.0)
-                nc.sync.dma_start(out=x_batch[0:LEFT_ROWS, TILES - 1, :], in_=left_source)
+
+        for b in range(BATCHES - LATE_LOADS):
+            load_batch(b)
 
         identity = consts.tile([P, P], F32)
         make_identity(nc, identity[:])
-
         w_codes = consts.tile([P, 2 * D_OUT], U32, align_bytes=64)
         w_scales = consts.tile([P, 2 * D_OUT], U8, align_bytes=64)
         bias = consts.tile([P, D_OUT], F32)
@@ -179,6 +168,9 @@ def tile_relativemultiheadattention_pa_t_kernel(tc, pos_embed, W_r, b_r, out):
                     out=grouped_words[:, t : t + FLIPPED_TILES],
                     in_=flipped[:].rearrange("p i u r -> p i r u"),
                 )
+            if (b, first + width) == (0, TILES):
+                features = grouped[:].rearrange("p (t r j) -> p t r j", r=P, j=PACK)
+                nc.vector.memset(features[:, width - ZERO_ROWS :, P - 1, :], 0.0)
             return grouped
 
         def quantise_group(g, grouped):
@@ -219,10 +211,13 @@ def tile_relativemultiheadattention_pa_t_kernel(tc, pos_embed, W_r, b_r, out):
                 done = slice(first, first + width)
                 nc.sync.dma_start(out=batch_target(b)[:, done, :], in_=keys[:, done, :])
             elif first + width == TILES:
-                nc.sync.dma_start(out=batch_target(b), in_=keys[:, 0 : whole_tiles(b), :])
+                nc.sync.dma_start(out=batch_target(b), in_=keys[:])
                 if b == 0:
-                    nc.sync.dma_start(out=left_target, in_=keys[0:LEFT_ROWS, TILES - 1, :])
-                    nc.sync.dma_start(out=zero_target, in_=keys[LEFT_ROWS:P, TILES - 1, :])
+                    nc.sync.dma_start(
+                        out=zero_target.unsqueeze(0), in_=keys[P - 1 :, TILES - ZERO_ROWS + 1 :, :]
+                    )
+                    for late in range(BATCHES - LATE_LOADS, BATCHES):
+                        load_batch(late)
 
         prepare_weights()
         scalar_spreads = {0: None}
@@ -238,7 +233,7 @@ def tile_relativemultiheadattention_pa_t_kernel(tc, pos_embed, W_r, b_r, out):
                 quantised_groups[g - 1] = quantise_group(g - 1, flipped_groups[g - 1])
             if g + 1 < n_groups:
                 vector_spreads[g + 1] = sort_on_vector(g + 1) if g + 1 < n_groups - 2 else None
-            if g == 1:
+            if g == 2:
                 prepare_bias()
             if g >= 2:
                 multiply_group(g - 2, *quantised_groups[g - 2])

@@ -27,6 +27,7 @@ SCALAR_SORTS = {8: 1, 4: 1}
 FLIPPED_TILES = BANK // (HALVES * P)
 PRODUCT_TILES = BANK // D_OUT
 
+SCALAR_STORES = {12: 1, 14: 3}
 LATE_LOADS = 2
 ZERO_ROWS = BATCHES - 1
 
@@ -91,7 +92,7 @@ def tile_relativemultiheadattention_pa_t_kernel(tc, pos_embed, W_r, b_r, out):
         def load_batch(b):
             x_batch = x_pool.tile([P, TILES, D_IN], BF16, name="x_batch")
             x_batches.append(x_batch)
-            edges = {0: (0, 4, 8, TILES), 1: (0, 8, TILES)}.get(b, (0, TILES))
+            edges = {0: (0, 4, 8, TILES), 1: (0, 8, TILES), 2: (0, 8, TILES)}.get(b, (0, TILES))
             for first, last in zip(edges, edges[1:]):
                 nc.sync.dma_start(out=x_batch[:, first:last, :], in_=batch_source(b)[:, first:last, :])
 
@@ -168,13 +169,13 @@ def tile_relativemultiheadattention_pa_t_kernel(tc, pos_embed, W_r, b_r, out):
                     out=grouped_words[:, t : t + FLIPPED_TILES],
                     in_=flipped[:].rearrange("p i u r -> p i r u"),
                 )
-            if (b, first + width) == (0, TILES):
-                features = grouped[:].rearrange("p (t r j) -> p t r j", r=P, j=PACK)
-                nc.vector.memset(features[:, width - ZERO_ROWS :, P - 1, :], 0.0)
             return grouped
 
         def quantise_group(g, grouped):
-            width = groups[g][2]
+            b, first, width = groups[g]
+            if (b, first + width) == (0, TILES):
+                features = grouped[:].rearrange("p (t r j) -> p t r j", r=P, j=PACK)
+                nc.vector.memset(features[:, width - ZERO_ROWS :, P - 1, :], 0.0)
             codes = mx_pool.tile([P, width * P], U32, align_bytes=64, name="codes")
             scales = mx_pool.tile([P, width * P], U8, align_bytes=64, name="scales")
             nc.vector.quantize_mx(out=codes[:].bitcast(FP8X4), scales=scales[:], in_=grouped[:])
@@ -210,7 +211,7 @@ def tile_relativemultiheadattention_pa_t_kernel(tc, pos_embed, W_r, b_r, out):
             if b == BATCHES - 1:
                 done = slice(first, first + width)
                 nc.sync.dma_start(out=batch_target(b)[:, done, :], in_=keys[:, done, :])
-            elif first + width == TILES:
+            elif first + width == TILES and b not in SCALAR_STORES.values():
                 nc.sync.dma_start(out=batch_target(b), in_=keys[:])
                 if b == 0:
                     nc.sync.dma_start(
@@ -235,5 +236,8 @@ def tile_relativemultiheadattention_pa_t_kernel(tc, pos_embed, W_r, b_r, out):
                 vector_spreads[g + 1] = sort_on_vector(g + 1) if g + 1 < n_groups - 2 else None
             if g == 2:
                 prepare_bias()
+            if g in SCALAR_STORES:
+                stored = SCALAR_STORES[g]
+                nc.scalar.dma_start(out=batch_target(stored), in_=keys_batches[stored][:])
             if g >= 2:
                 multiply_group(g - 2, *quantised_groups[g - 2])

@@ -27,7 +27,6 @@ SCALAR_SORTS = {8: 1, 4: 1}
 FLIPPED_TILES = BANK // (HALVES * P)
 PRODUCT_TILES = BANK // D_OUT
 
-SCALAR_STORES = {12: 1, 14: 3}
 LATE_LOADS = 2
 ZERO_ROWS = BATCHES - 1
 
@@ -84,8 +83,6 @@ def tile_relativemultiheadattention_pa_t_kernel(tc, pos_embed, W_r, b_r, out):
         nc.vector.memset(ones[:], 1.0)
         bias_rows = consts.tile([P, D_OUT], BF16)
         nc.vector.memset(bias_rows[:], 0.0)
-        nc.scalar.dma_start(out=bias_rows[0:1, :], in_=b_r.unsqueeze(0))
-
         nc.sync.dma_start(out=w_raw[:], in_=W_r)
         x_batches = []
 
@@ -96,7 +93,9 @@ def tile_relativemultiheadattention_pa_t_kernel(tc, pos_embed, W_r, b_r, out):
             for first, last in zip(edges, edges[1:]):
                 nc.sync.dma_start(out=x_batch[:, first:last, :], in_=batch_source(b)[:, first:last, :])
 
-        for b in range(BATCHES - LATE_LOADS):
+        load_batch(0)
+        nc.sync.dma_start(out=bias_rows[0:1, :], in_=b_r.unsqueeze(0))
+        for b in range(1, BATCHES - LATE_LOADS):
             load_batch(b)
 
         identity = consts.tile([P, P], F32)
@@ -208,10 +207,10 @@ def tile_relativemultiheadattention_pa_t_kernel(tc, pos_embed, W_r, b_r, out):
                     in0=product[:],
                     in1=bias[:].unsqueeze(1).to_broadcast([P, PRODUCT_TILES, D_OUT]),
                 )
-            if b == BATCHES - 1:
-                done = slice(first, first + width)
+            if b == BATCHES - 1 and first > 0:
+                done = slice(0, first + width) if first == GROUP else slice(first, first + width)
                 nc.sync.dma_start(out=batch_target(b)[:, done, :], in_=keys[:, done, :])
-            elif first + width == TILES and b not in SCALAR_STORES.values():
+            elif b < BATCHES - 1 and first + width == TILES:
                 nc.sync.dma_start(out=batch_target(b), in_=keys[:])
                 if b == 0:
                     nc.sync.dma_start(
@@ -236,8 +235,5 @@ def tile_relativemultiheadattention_pa_t_kernel(tc, pos_embed, W_r, b_r, out):
                 vector_spreads[g + 1] = sort_on_vector(g + 1) if g + 1 < n_groups - 2 else None
             if g == 2:
                 prepare_bias()
-            if g in SCALAR_STORES:
-                stored = SCALAR_STORES[g]
-                nc.scalar.dma_start(out=batch_target(stored), in_=keys_batches[stored][:])
             if g >= 2:
                 multiply_group(g - 2, *quantised_groups[g - 2])

from contextlib import ExitStack

import concourse.mybir as mybir
from concourse.masks import make_identity

BF16 = mybir.dt.bfloat16
F32 = mybir.dt.float32
U32 = mybir.dt.uint32
U8 = mybir.dt.uint8
FP8X4 = mybir.dt.float8_e4m3fn_x4

P = 128
BATCHES = 8
SEQ = 2048
D_IN = 512
D_OUT = 128
PACK = 4
BANK = 512

RUN = 8
HALVES = D_IN // 2 // P
TILES = SEQ // P
GROUP = 8
GROUP_WIDTHS = {0: (4, 4, 8), BATCHES - 1: (8, 4, 4)}
VECTOR_SORTS = {8: 2, 4: 1}
SCALAR_SORTS = {8: 1, 4: 1}
FLIPPED_TILES = BANK // (HALVES * P)
PRODUCT_TILES = BANK // D_OUT

LATE_LOADS = 2
ZERO_ROWS = BATCHES - 1

FLOPS = 2 * BATCHES * SEQ * D_IN * D_OUT


def transpose_row_tile(nc, identity, flipped, row_tile):
    words = row_tile.bitcast(F32)
    for u in range(HALVES):
        nc.tensor.transpose(flipped[:, u, :], words[:, u::HALVES], identity)


def sort_words(copy, spread, row_tiles):
    words = row_tiles.rearrange("p t k -> p (t k)").bitcast(F32)
    copy(
        out=spread.rearrange("p u (n i) -> p u n i", i=RUN),
        in_=words.rearrange("p (n u i) -> p u n i", u=HALVES, i=RUN),
    )


def transpose_sorted_tile(nc, identity, flipped, spread, t):
    for u in range(HALVES):
        nc.tensor.transpose(flipped[:, u, :], spread[:, u, t * P : (t + 1) * P], identity)


def tile_relativemultiheadattention_pa_t_kernel(tc, pos_embed, W_r, b_r, out):
    nc = tc.nc
    pos_rows = pos_embed.flatten_outer_dims()
    out_rows = out.flatten_outer_dims()

    def batch_source(b):
        first = ZERO_ROWS if b == 0 else SEQ * b
        return pos_rows[first : first + SEQ, :].rearrange("(p t) k -> p t k", t=TILES)

    def batch_target(b):
        first = 0 if b == 0 else (SEQ + 1) * b - ZERO_ROWS
        return out_rows[first : first + SEQ, :].rearrange("(p t) d -> p t d", t=TILES)

    zero_target = out_rows[SEQ - ZERO_ROWS :, :].rearrange("(i r) d -> i r d", r=SEQ + 1)[1:, 0, :]

    with ExitStack() as ctx:
        consts = ctx.enter_context(tc.tile_pool(name="consts", bufs=1))
        x_pool = ctx.enter_context(tc.tile_pool(name="x", bufs=BATCHES - 1))
        grouped_pool = ctx.enter_context(tc.tile_pool(name="grouped", bufs=3))
        spread_pool = ctx.enter_context(tc.tile_pool(name="spread", bufs=2))
        mx_pool = ctx.enter_context(tc.tile_pool(name="mx", bufs=2))
        keys_pool = ctx.enter_context(tc.tile_pool(name="keys", bufs=BATCHES))
        flipped_pool = ctx.enter_context(tc.psum_pool(name="flipped", bufs=6))
        product_pool = ctx.enter_context(tc.psum_pool(name="product", bufs=2))
        ctx.enter_context(tc.manual_schedule())

        w_raw = consts.tile([P, D_IN], BF16)
        ones = consts.tile([P, P], BF16)
        nc.vector.memset(ones[:], 1.0)
        bias_rows = consts.tile([P, D_OUT], BF16)
        nc.vector.memset(bias_rows[:], 0.0)
        nc.sync.dma_start(out=w_raw[:], in_=W_r)
        x_batches = []

        def load_batch(b):
            x_batch = x_pool.tile([P, TILES, D_IN], BF16, name="x_batch")
            x_batches.append(x_batch)
            edges = {0: (0, 4, 8, TILES), 1: (0, 8, TILES), 2: (0, 8, TILES)}.get(b, (0, TILES))
            for first, last in zip(edges, edges[1:]):
                nc.sync.dma_start(out=x_batch[:, first:last, :], in_=batch_source(b)[:, first:last, :])

        load_batch(0)
        nc.sync.dma_start(out=bias_rows[0:1, :], in_=b_r.unsqueeze(0))
        for b in range(1, BATCHES - LATE_LOADS):
            load_batch(b)

        identity = consts.tile([P, P], F32)
        make_identity(nc, identity[:])
        w_codes = consts.tile([P, 2 * D_OUT], U32, align_bytes=64)
        w_scales = consts.tile([P, 2 * D_OUT], U8, align_bytes=64)
        bias = consts.tile([P, D_OUT], F32)

        def prepare_weights():
            w_spread = consts.tile([P, HALVES, P], F32, name="w_spread")
            sort_words(nc.vector.tensor_copy, w_spread[:], w_raw[:].unsqueeze(1))
            w_flipped = flipped_pool.tile([P, FLIPPED_TILES, HALVES, P], F32, name="flipped")
            transpose_row_tile(nc, identity[:], w_flipped[:, 0], w_raw[:])
            transpose_sorted_tile(nc, identity[:], w_flipped[:, 1], w_spread[:], 0)
            w_grouped = consts.tile([P, 2 * D_OUT * PACK], BF16, align_bytes=64, name="w_grouped")
            nc.scalar.copy(
                out=w_grouped[:].bitcast(F32).rearrange("p (i r u) -> p i r u", i=2, u=HALVES),
                in_=w_flipped[:].rearrange("p i u r -> p i r u"),
            )
            nc.vector.quantize_mx(out=w_codes[:].bitcast(FP8X4), scales=w_scales[:], in_=w_grouped[:])

        def prepare_bias():
            bias_product = product_pool.tile([P, PRODUCT_TILES, D_OUT], F32, name="product")
            nc.tensor.matmul(out=bias_product[:, 0, :], lhsT=ones[:], rhs=bias_rows[:], start=True, stop=True)
            nc.vector.tensor_copy(out=bias[:], in_=bias_product[:, 0, :])

        groups = []
        for b in range(BATCHES):
            first = 0
            for width in GROUP_WIDTHS.get(b, (GROUP, GROUP)):
                groups.append((b, first, width))
                first += width
        n_groups = len(groups)

        def sorted_from(g):
            width = groups[g][2]
            by_vector = width - (VECTOR_SORTS[width] if g < n_groups - 2 else 0)
            return by_vector - SCALAR_SORTS[width], by_vector

        def sort_on_scalar(g):
            b, first, width = groups[g]
            by_scalar, by_vector = sorted_from(g)
            spread = spread_pool.tile([P, HALVES, (by_vector - by_scalar) * P], F32, name="scalar_spread")
            sort_words(nc.scalar.copy, spread[:], x_batches[b][:, first + by_scalar : first + by_vector, :])
            return spread

        def sort_on_vector(g):
            b, first, width = groups[g]
            by_vector = sorted_from(g)[1]
            spread = spread_pool.tile([P, HALVES, (width - by_vector) * P], F32, name="vector_spread")
            sort_words(nc.vector.tensor_copy, spread[:], x_batches[b][:, first + by_vector : first + width, :])
            return spread

        def flip_group(g, scalar_spread, vector_spread):
            b, first, width = groups[g]
            x_batch = x_batches[b]
            by_scalar, by_vector = sorted_from(g) if g else (width, width)
            grouped = grouped_pool.tile([P, width * P * PACK], BF16, align_bytes=64, name="grouped")
            grouped_words = grouped[:].bitcast(F32).rearrange("p (t r u) -> p t r u", r=P, u=HALVES)
            for t in range(0, width, FLIPPED_TILES):
                flipped = flipped_pool.tile([P, FLIPPED_TILES, HALVES, P], F32, name="flipped")
                for i in range(FLIPPED_TILES):
                    if t + i >= by_vector:
                        transpose_sorted_tile(nc, identity[:], flipped[:, i], vector_spread, t + i - by_vector)
                    elif t + i >= by_scalar:
                        transpose_sorted_tile(nc, identity[:], flipped[:, i], scalar_spread, t + i - by_scalar)
                    else:
                        transpose_row_tile(nc, identity[:], flipped[:, i], x_batch[:, first + t + i, :])
                nc.scalar.copy(
                    out=grouped_words[:, t : t + FLIPPED_TILES],
                    in_=flipped[:].rearrange("p i u r -> p i r u"),
                )
            return grouped

        def quantise_group(g, grouped):
            b, first, width = groups[g]
            if (b, first + width) == (0, TILES):
                features = grouped[:].rearrange("p (t r j) -> p t r j", r=P, j=PACK)
                nc.vector.memset(features[:, width - ZERO_ROWS :, P - 1, :], 0.0)
            codes = mx_pool.tile([P, width * P], U32, align_bytes=64, name="codes")
            scales = mx_pool.tile([P, width * P], U8, align_bytes=64, name="scales")
            nc.vector.quantize_mx(out=codes[:].bitcast(FP8X4), scales=scales[:], in_=grouped[:])
            return codes, scales

        keys_batches = []

        def multiply_group(g, codes, scales):
            b, first, width = groups[g]
            by_scalar = sorted_from(g)[0] if g else width
            if first == 0:
                keys_batches.append(keys_pool.tile([P, TILES, D_OUT], F32, name="keys"))
            keys = keys_batches[b]
            for t in range(0, width, PRODUCT_TILES):
                product = product_pool.tile([P, PRODUCT_TILES, D_OUT], F32, name="product")
                for i in range(PRODUCT_TILES):
                    rows = slice((t + i) * P, (t + i + 1) * P)
                    w_columns = slice(D_OUT, 2 * D_OUT) if t + i >= by_scalar else slice(0, D_OUT)
                    nc.tensor.matmul_mx(
                        out=product[:, i, :],
                        lhsT=codes[:, rows].bitcast(FP8X4),
                        lhsT_scale=scales[:, rows],
                        rhs=w_codes[:, w_columns].bitcast(FP8X4),
                        rhs_scale=w_scales[:, w_columns],
                        start=True,
                        stop=True,
                    )
                nc.vector.tensor_add(
                    out=keys[:, first + t : first + t + PRODUCT_TILES, :],
                    in0=product[:],
                    in1=bias[:].unsqueeze(1).to_broadcast([P, PRODUCT_TILES, D_OUT]),
                )
            if b == BATCHES - 1 and first > 0:
                done = slice(0, first + width) if first == GROUP else slice(first, first + width)
                nc.sync.dma_start(out=batch_target(b)[:, done, :], in_=keys[:, done, :])
            elif b < BATCHES - 1 and first + width == TILES:
                nc.sync.dma_start(out=batch_target(b), in_=keys[:])
                if b == 0:
                    nc.sync.dma_start(
                        out=zero_target.unsqueeze(0), in_=keys[P - 1 :, TILES - ZERO_ROWS + 1 :, :]
                    )
                    for late in range(BATCHES - LATE_LOADS, BATCHES):
                        load_batch(late)

        prepare_weights()
        scalar_spreads = {0: None}
        vector_spreads = {0: None}
        flipped_groups = {}
        quantised_groups = {}
        for g in range(n_groups + 2):
            if g < n_groups:
                flipped_groups[g] = flip_group(g, scalar_spreads[g], vector_spreads[g])
            if g + 1 < n_groups:
                scalar_spreads[g + 1] = sort_on_scalar(g + 1)
            if 1 <= g <= n_groups:
                quantised_groups[g - 1] = quantise_group(g - 1, flipped_groups[g - 1])
            if g + 1 < n_groups:
                vector_spreads[g + 1] = sort_on_vector(g + 1) if g + 1 < n_groups - 2 else None
            if g == 2:
                prepare_bias()
            if g >= 2:
                multiply_group(g - 2, *quantised_groups[g - 2])
